import numpy as np
import ml_dtypes


def mxq(x, axis, fmt="e4m3"):
    dtype, down = {"e4m3": (ml_dtypes.float8_e4m3fn, 7), "e5m2": (ml_dtypes.float8_e5m2, 14)}[fmt]
    v = np.moveaxis(np.asarray(x, np.float32).astype(ml_dtypes.bfloat16).astype(np.float64), axis, -1)
    blocks = v.reshape(v.shape[:-1] + (-1, 32))
    amax = np.abs(blocks).max(-1, keepdims=True)
    byte = np.maximum(np.where(amax > 0, np.frexp(amax)[1] - 1 + 127, 0) - down, 1)
    scale = np.exp2(byte - 127.0)
    codes = (blocks / scale).astype(np.float32).astype(dtype).astype(np.float64)
    return np.moveaxis((codes * scale).reshape(v.shape), -1, axis)


WIDE = False


def mx_kscale(k):
    if not WIDE:
        return np.ones(k)
    levels = np.array([30, -30])
    if k % 512:
        return np.exp2(np.random.permutation(np.resize(levels, k // 32))).repeat(32)
    a = np.empty((k // 512, 16))
    for p in range(k // 512):
        a[p, :8] = np.random.permutation(np.resize(levels, 8))
        for g in range(8):
            far = levels[np.abs(levels - a[p, g]) >= 10]
            a[p, g + 8] = far[np.random.randint(len(far))]
    return np.exp2(a.ravel()).repeat(32)


BF16 = ml_dtypes.bfloat16


def bf(x):
    return np.asarray(x, np.float32).astype(BF16)


def f64(x):
    return np.asarray(x).astype(np.float64)


B, S, T, E, D, H = 1, 512, 512, 2048, 2048, 16
DK = D // H


def rope_tables(n):
    m = np.arange(n, dtype=np.float64)[:, None]
    i = np.repeat(np.arange(DK // 2, dtype=np.float64), 2)[None, :]
    ang = m * np.exp(-(2.0 * np.log(1e4) / DK) * i)
    return np.cos(ang), np.sin(ang)


def rotate_pairs(x):
    return np.stack([-x[..., 1::2], x[..., 0::2]], axis=-1).reshape(x.shape)


def setup_inputs():
    s = mx_kscale(E)
    return {"x": bf(np.random.standard_normal((B, S, E)) * s),
            "w": bf(np.random.standard_normal((E, D)) * 1.1 / np.sqrt(E) / s[:, None]),
            "b": bf(np.random.standard_normal(D) * 0.4)}


def reference(x, w, b):
    p = (mxq(f64(x), 2, "e5m2") @ mxq(f64(w), 0, "e4m3")) + f64(b)
    p = p.reshape(B, S, H, DK).transpose(0, 2, 1, 3)
    r1, r2 = rope_tables(S)
    return p * r1 + rotate_pairs(p) * r2

@@ -1,0 +1,241 @@
+from contextlib import ExitStack
+
+import concourse.mybir as mybir
+from concourse.masks import make_identity
+
+F32 = mybir.dt.float32
+BF16 = mybir.dt.bfloat16
+I32 = mybir.dt.int32
+U32 = mybir.dt.uint32
+U8 = mybir.dt.uint8
+E4X4 = mybir.dt.float8_e4m3fn_x4
+E5X4 = mybir.dt.float8_e5m2_x4
+ALU = mybir.AluOpType
+ACT = mybir.ActivationFunctionType
+
+P = 128
+S_TOK = 512
+K = 2048
+D = 2048
+H = 16
+PASSES = 4
+PI = 3.141592653589793
+FLOPS = 2 * S_TOK * K * D
+
+S_W = 90
+GROUP_W = (256, 256, 512, 1024)
+
+
+def tile_multiheadedattention_pa_kernel(tc, x, w, b, out):
+    nc = tc.nc
+    with ExitStack() as ctx:
+        const = ctx.enter_context(tc.tile_pool(name="const", bufs=1))
+        wrawp = ctx.enter_context(tc.tile_pool(name="wrawp", bufs=1))
+        gwp = ctx.enter_context(tc.tile_pool(name="gwp", bufs=3))
+        wqp = ctx.enter_context(tc.tile_pool(name="wqp", bufs=3))
+        epi = ctx.enter_context(tc.tile_pool(name="epi", bufs=3))
+        psum = ctx.enter_context(tc.psum_pool(name="psum", bufs=1))
+        ctx.enter_context(tc.manual_schedule())
+
+        xv = x.flatten_outer_dims().rearrange("(r a) k -> r a k", a=4)
+        xs = const.tile([P, 4, K], BF16, name="xs")
+        bias = const.tile([P, H], BF16, name="bias")
+        with nc.allow_non_contiguous_dma(reason="bias, one element a partition"):
+            nc.scalar.dma_start(out=bias[:], in_=b.rearrange("(h j) -> j h", j=P))
+        wv = w.rearrange("(c p j) d -> c p j d", p=P, j=4)
+        wg = []
+        place = []
+        col0 = 0
+        for g in range(len(GROUP_W)):
+            t = wrawp.tile([P, PASSES, 4, GROUP_W[g]], BF16, name="wg%d" % g)
+            wg.append(t)
+            for c in range(PASSES):
+                if g == 0:
+                    nc.sync.dma_start(out=xs[:, :, 512 * c:512 * (c + 1)], in_=xv[:, :, 512 * c:512 * (c + 1)])
+                nc.sync.dma_start(out=t[:, c, :, :], in_=wv[c, :, :, col0:col0 + GROUP_W[g]])
+            for o in range(0, GROUP_W[g], P):
+                place.append((g, o))
+            col0 += GROUP_W[g]
+
+        zero1 = const.tile([P, 1], F32, name="zero1")
+        nc.vector.memset(zero1[:], 0.0)
+        warm = const.tile([P, 1], F32, name="warm")
+        nc.scalar.activation(out=warm[:], in_=zero1[:], func=ACT.Sin)
+
+        jcol = const.tile([P, 1], I32, name="jcol")
+        nc.gpsimd.iota(jcol[:], pattern=[[0, 1]], base=0, channel_multiplier=1)
+        ident = const.tile([P, P], F32, name="ident")
+        make_identity(nc, ident[:])
+        mi = const.tile([P, S_TOK], F32, name="mi")
+        nc.gpsimd.iota(mi[:], pattern=[[1, 4], [4, P]], base=0, channel_multiplier=0,
+                       allow_small_or_imprecise_dtypes=True)
+        psw = const.tile([P, P], F32, name="psw")
+        iv = ident[:].rearrange("p (i e) -> p i e", e=2)
+        pv = psw[:].rearrange("p (i e) -> p i e", e=2)
+        nc.gpsimd.tensor_copy(out=pv[:, :, 0:1], in_=iv[:, :, 1:2])
+        nc.gpsimd.tensor_copy(out=pv[:, :, 1:2], in_=iv[:, :, 0:1])
+
+        bits = const.tile([P, 8], I32, name="bits")
+        for k in range(7):
+            nc.vector.tensor_scalar(out=bits[:, k:k + 1], in0=jcol[:], scalar1=k, scalar2=1,
+                                    op0=ALU.logical_shift_right, op1=ALU.bitwise_and)
+        bitsf = const.tile([P, 8], F32, name="bitsf")
+        nc.vector.tensor_copy(out=bitsf[:, 0:7], in_=bits[:, 0:7])
+        fac = const.tile([P, 8], F32, name="fac")
+        for k in range(1, 7):
+            ck = 10.0 ** (-(2.0 ** (k - 1)) / 16.0)
+            s0 = 1.0 / (2.0 * PI) if k == 1 else 1.0
+            nc.vector.tensor_scalar(out=fac[:, k:k + 1], in0=bitsf[:, k:k + 1], scalar1=(ck - 1.0) * s0,
+                                    scalar2=s0, op0=ALU.mult, op1=ALU.add)
+        nc.vector.tensor_scalar(out=fac[:, 0:1], in0=bitsf[:, 0:1], scalar1=-4.0 * PI, scalar2=2.0 * PI,
+                                op0=ALU.mult, op1=ALU.add)
+        turns = const.tile([P, 4], F32, name="turns")
+        nc.vector.tensor_scalar(out=turns[:, 0:1], in0=fac[:, 1:2], scalar1=fac[:, 2:3], scalar2=fac[:, 3:4],
+                                op0=ALU.mult, op1=ALU.mult)
+        nc.vector.tensor_scalar(out=turns[:, 1:2], in0=turns[:, 0:1], scalar1=fac[:, 4:5], scalar2=fac[:, 5:6],
+                                op0=ALU.mult, op1=ALU.mult)
+        nc.vector.tensor_scalar(out=turns[:, 2:3], in0=turns[:, 1:2], scalar1=fac[:, 6:7], scalar2=None,
+                                op0=ALU.mult)
+        u = turns[:, 2:3]
+
+        fr = const.tile([P, 2 * S_TOK], F32, name="fr")
+        ni = const.tile([P, 2 * S_TOK], I32, name="ni")
+        nf = const.tile([P, 2 * S_TOK], F32, name="nf")
+        for e in range(2):
+            half = slice(S_TOK * e, S_TOK * (e + 1))
+            nc.vector.tensor_scalar(out=ni[:, half], in0=mi[:], scalar1=u, scalar2=0.25 * e, op0=ALU.mult, op1=ALU.add)
+            nc.vector.tensor_scalar(out=nf[:, half], in0=ni[:, half], scalar1=-0.25 * e, scalar2=None, op0=ALU.add)
+            nc.vector.scalar_tensor_tensor(out=fr[:, half], in0=mi[:], scalar=u, in1=nf[:, half],
+                                           op0=ALU.mult, op1=ALU.subtract)
+        sin_t = const.tile([P, S_TOK], F32, name="sin_t")
+        cos_t = const.tile([P, S_TOK], F32, name="cos_t")
+
+        gx = []
+        for c in range(PASSES):
+            g = const.tile([P, 4 * S_TOK], BF16, name="gx%d" % c, align_bytes=64)
+            gx.append(g)
+        xq = const.tile([P, PASSES, S_TOK], U32, name="xq", align_bytes=64)
+        xsc = const.tile([P, PASSES, S_TOK], U8, name="xsc", align_bytes=64)
+        outv = out.rearrange("o h (r a) j -> (o h) r (a j)", a=4)
+        blocks = {}
+        accs = {}
+        uvs = {}
+        os_ = {}
+
+        def bank(shape, name):
+            return psum.tile(shape, F32, name=name, tag="bank", bufs=8)
+
+        def x_pass(c):
+            for ap in range(2):
+                xt = bank([P, 2, 2, P], "xt")
+                for a2 in range(2):
+                    words = xs[:, 2 * ap + a2, :].bitcast(F32)
+                    for uu in range(2):
+                        nc.tensor.transpose(xt[:, a2, uu, :], words[:, 256 * c + uu:256 * (c + 1):2], ident[:])
+                dst = gx[c][:].bitcast(F32)[:, 512 * ap:512 * (ap + 1)].rearrange("p (a r u) -> p a r u", a=2, u=2)
+                src = xt[:].rearrange("p a u r -> p a r u")
+                if ap == 0:
+                    nc.scalar.copy(out=dst, in_=src)
+                else:
+                    nc.vector.tensor_copy(out=dst, in_=src)
+
+        def x_quant(c):
+            nc.vector.quantize_mx(out=xq[:, c, :].bitcast(E5X4), scales=xsc[:, c, :], in_=gx[c][:])
+
+        def new_block(first, heads):
+            gw = gwp.tile([P, PASSES, heads * P, 4], BF16, name="gw%d" % heads, align_bytes=64)
+            wq = wqp.tile([P, PASSES, heads * P], U32, name="wq%d" % heads, align_bytes=64)
+            wsc = wqp.tile([P, PASSES, heads * P], U8, name="wsc%d" % heads, align_bytes=64)
+            for i in range(heads):
+                blocks[first + i] = (gw, wq, wsc, first, heads)
+
+        def interleave(h, cs):
+            gw, wq, wsc, first, heads = blocks[h]
+            g, o = place[first]
+            src = wg[g][:, cs, :, o:o + heads * P]
+            cut = heads * S_W
+            nc.scalar.copy(out=gw[:, cs, 0:cut, :], in_=src[:, :, :, 0:cut].rearrange("p c j w -> p c w j"))
+            nc.vector.tensor_copy(out=gw[:, cs, cut:, :], in_=src[:, :, :, cut:].rearrange("p c j w -> p c w j"))
+
+        def quant(h, cs):
+            gw, wq, wsc, first, heads = blocks[h]
+            nc.vector.quantize_mx(out=wq[:, cs, :].rearrange("p c w -> p (c w)").bitcast(E4X4),
+                                  scales=wsc[:, cs, :].rearrange("p c w -> p (c w)"),
+                                  in_=gw[:, cs, :, :].rearrange("p c w j -> p (c w j)"))
+
+        def mx(h, c):
+            gw, wq, wsc, first, heads = blocks[h]
+            cols = slice(P * (h - first), P * (h - first + 1))
+            if c == 0:
+                accs[h] = bank([P, S_TOK], "acc")
+            nc.tensor.matmul_mx(out=accs[h][:],
+                                lhsT=wq[:, c, cols].bitcast(E4X4), lhsT_scale=wsc[:, c, cols],
+                                rhs=xq[:, c, :].bitcast(E5X4), rhs_scale=xsc[:, c, :],
+                                start=(c == 0), stop=(c == PASSES - 1))
+
+        def epi_u(h):
+            ut = epi.tile([P, S_TOK], F32, name="ut")
+            nc.vector.scalar_tensor_tensor(out=ut[:], in0=accs[h][:], scalar=bias[:, h:h + 1], in1=cos_t[:],
+                                           op0=ALU.add, op1=ALU.mult)
+            uvs[h] = [ut]
+
+        def epi_v(h):
+            vt = epi.tile([P, S_TOK], F32, name="vt")
+            nc.vector.scalar_tensor_tensor(out=vt[:], in0=accs[h][:], scalar=bias[:, h:h + 1], in1=sin_t[:],
+                                           op0=ALU.add, op1=ALU.mult)
+            uvs[h].append(vt)
+
+        def epi_pe(h):
+            ut, vt = uvs[h]
+            o = bank([P, 4, P], "o")
+            for a in range(4):
+                nc.tensor.matmul(out=o[:, a, :], lhsT=ut[:, P * a:P * (a + 1)], rhs=ident[:],
+                                 start=True, stop=False, is_transpose=True)
+                nc.tensor.matmul(out=o[:, a, :], lhsT=vt[:, P * a:P * (a + 1)], rhs=psw[:],
+                                 start=False, stop=True, is_transpose=True)
+            os_[h] = o
+
+        def epi_s(h):
+            res = epi.tile([P, S_TOK], F32, name="res")
+            nc.scalar.copy(out=res[:], in_=os_[h][:].rearrange("p a j -> p (a j)"))
+            nc.sync.dma_start(out=outv[h], in_=res[:])
+
+        new_block(0, 2)
+        new_block(2, 2)
+        for k in range(9):
+            if k < PASSES:
+                x_pass(k)
+            if k < 8:
+                interleave(2 * (k // PASSES), slice(k % PASSES, k % PASSES + 1))
+            if k == 6:
+                epi_u(0)
+            if 1 <= k <= PASSES:
+                x_quant(k - 1)
+            if k >= 1:
+                first, c = 2 * ((k - 1) // PASSES), (k - 1) % PASSES
+                quant(first, slice(c, c + 1))
+                mx(first, c)
+                mx(first + 1, c)
+            if k == 7:
+                epi_v(0)
+            if k == 2:
+                nc.scalar.activation(out=sin_t[:], in_=fr[:, 0:S_TOK], func=ACT.Sin, scale=fac[:, 0:1])
+                nc.scalar.activation(out=cos_t[:], in_=fr[:, S_TOK:], func=ACT.Sin, scale=2.0 * PI)
+        every = slice(0, PASSES)
+        for t in range(4, H + 6):
+            if t < H:
+                new_block(t, 1)
+                interleave(t, every)
+            if t - 3 < H:
+                epi_u(t - 3)
+            if 4 <= t - 1 < H:
+                quant(t - 1, every)
+            if t - 3 < H:
+                epi_v(t - 3)
+            if 4 <= t - 2 < H:
+                for c in range(PASSES):
+                    mx(t - 2, c)
+            if t - 4 < H:
+                epi_pe(t - 4)
+            if 0 <= t - 5 < H:
+                epi_s(t - 5)

@@ -23,7 +23,7 @@ PI = 3.141592653589793
 FLOPS = 2 * S_TOK * K * D
 
 S_W = 90
-GROUP_W = (256, 256, 512, 1024)
+GROUP_W = (256, 256, 256, 256, 512, 512)
 
 
 def tile_multiheadedattention_pa_kernel(tc, x, w, b, out):
@@ -134,10 +134,7 @@ def tile_multiheadedattention_pa_kernel(tc, x, w, b, out):
                         nc.tensor.transpose(xt[:, a2, uu, :], words[:, 256 * c + uu:256 * (c + 1):2], ident[:])
                 dst = gx[c][:].bitcast(F32)[:, 512 * ap:512 * (ap + 1)].rearrange("p (a r u) -> p a r u", a=2, u=2)
                 src = xt[:].rearrange("p a u r -> p a r u")
-                if ap == 0:
-                    nc.scalar.copy(out=dst, in_=src)
-                else:
-                    nc.vector.tensor_copy(out=dst, in_=src)
+                nc.scalar.copy(out=dst, in_=src)
 
         def x_quant(c):
             nc.vector.quantize_mx(out=xq[:, c, :].bitcast(E5X4), scales=xsc[:, c, :], in_=gx[c][:])

@@ -38,7 +38,7 @@ def tile_multiheadedattention_pa_kernel(tc, x, w, b, out):
         ctx.enter_context(tc.manual_schedule())
 
         xv = x.flatten_outer_dims().rearrange("(r a) k -> r a k", a=4)
-        xs = const.tile([P, 4, K], BF16, name="xs")
+        xs = []
         bias = const.tile([P, H], BF16, name="bias")
         with nc.allow_non_contiguous_dma(reason="bias, one element a partition"):
             nc.scalar.dma_start(out=bias[:], in_=b.rearrange("(h j) -> j h", j=P))
@@ -50,9 +50,11 @@ def tile_multiheadedattention_pa_kernel(tc, x, w, b, out):
             t = wrawp.tile([P, PASSES, 4, GROUP_W[g]], BF16, name="wg%d" % g)
             wg.append(t)
             for c in range(PASSES):
-                if g == 0:
-                    nc.sync.dma_start(out=xs[:, :, 512 * c:512 * (c + 1)], in_=xv[:, :, 512 * c:512 * (c + 1)])
                 nc.sync.dma_start(out=t[:, c, :, :], in_=wv[c, :, :, col0:col0 + GROUP_W[g]])
+                if g == 0:
+                    xc = const.tile([P, 4, 512], BF16, name="xs%d" % c)
+                    nc.sync.dma_start(out=xc[:], in_=xv[:, :, 512 * c:512 * (c + 1)])
+                    xs.append(xc)
             for o in range(0, GROUP_W[g], P):
                 place.append((g, o))
             col0 += GROUP_W[g]
@@ -64,11 +66,11 @@ def tile_multiheadedattention_pa_kernel(tc, x, w, b, out):
 
         jcol = const.tile([P, 1], I32, name="jcol")
         nc.gpsimd.iota(jcol[:], pattern=[[0, 1]], base=0, channel_multiplier=1)
-        ident = const.tile([P, P], F32, name="ident")
-        make_identity(nc, ident[:])
         mi = const.tile([P, S_TOK], F32, name="mi")
         nc.gpsimd.iota(mi[:], pattern=[[1, 4], [4, P]], base=0, channel_multiplier=0,
                        allow_small_or_imprecise_dtypes=True)
+        ident = const.tile([P, P], F32, name="ident")
+        make_identity(nc, ident[:])
         psw = const.tile([P, P], F32, name="psw")
         iv = ident[:].rearrange("p (i e) -> p i e", e=2)
         pv = psw[:].rearrange("p (i e) -> p i e", e=2)
@@ -107,8 +109,7 @@ def tile_multiheadedattention_pa_kernel(tc, x, w, b, out):
             nc.vector.tensor_scalar(out=nf[:, half], in0=ni[:, half], scalar1=-0.25 * e, scalar2=None, op0=ALU.add)
             nc.vector.scalar_tensor_tensor(out=fr[:, half], in0=mi[:], scalar=u, in1=nf[:, half],
                                            op0=ALU.mult, op1=ALU.subtract)
-        sin_t = const.tile([P, S_TOK], F32, name="sin_t")
-        cos_t = const.tile([P, S_TOK], F32, name="cos_t")
+        cs_t = const.tile([P, 2, S_TOK], F32, name="cs_t")
 
         gx = []
         for c in range(PASSES):
@@ -129,9 +130,9 @@ def tile_multiheadedattention_pa_kernel(tc, x, w, b, out):
             for ap in range(2):
                 xt = bank([P, 2, 2, P], "xt")
                 for a2 in range(2):
-                    words = xs[:, 2 * ap + a2, :].bitcast(F32)
+                    words = xs[c][:, 2 * ap + a2, :].bitcast(F32)
                     for uu in range(2):
-                        nc.tensor.transpose(xt[:, a2, uu, :], words[:, 256 * c + uu:256 * (c + 1):2], ident[:])
+                        nc.tensor.transpose(xt[:, a2, uu, :], words[:, uu:256:2], ident[:])
                 dst = gx[c][:].bitcast(F32)[:, 512 * ap:512 * (ap + 1)].rearrange("p (a r u) -> p a r u", a=2, u=2)
                 src = xt[:].rearrange("p a u r -> p a r u")
                 nc.scalar.copy(out=dst, in_=src)
@@ -150,9 +151,14 @@ def tile_multiheadedattention_pa_kernel(tc, x, w, b, out):
             gw, wq, wsc, first, heads = blocks[h]
             g, o = place[first]
             src = wg[g][:, cs, :, o:o + heads * P]
-            cut = heads * S_W
-            nc.scalar.copy(out=gw[:, cs, 0:cut, :], in_=src[:, :, :, 0:cut].rearrange("p c j w -> p c w j"))
-            nc.vector.tensor_copy(out=gw[:, cs, cut:, :], in_=src[:, :, :, cut:].rearrange("p c j w -> p c w j"))
+            if cs.stop - cs.start == 1:
+                cut = heads * S_W
+                nc.scalar.copy(out=gw[:, cs, 0:cut, :], in_=src[:, :, :, 0:cut].rearrange("p c j w -> p c w j"))
+                nc.vector.tensor_copy(out=gw[:, cs, cut:, :], in_=src[:, :, :, cut:].rearrange("p c j w -> p c w j"))
+            else:
+                ns = 2 if h % 4 == 3 else 3
+                nc.scalar.copy(out=gw[:, 0:ns, :, :], in_=src[:, 0:ns, :, :].rearrange("p c j w -> p c w j"))
+                nc.vector.tensor_copy(out=gw[:, ns:, :, :], in_=src[:, ns:, :, :].rearrange("p c j w -> p c w j"))
 
         def quant(h, cs):
             gw, wq, wsc, first, heads = blocks[h]
@@ -170,25 +176,19 @@ def tile_multiheadedattention_pa_kernel(tc, x, w, b, out):
                                 rhs=xq[:, c, :].bitcast(E5X4), rhs_scale=xsc[:, c, :],
                                 start=(c == 0), stop=(c == PASSES - 1))
 
-        def epi_u(h):
-            ut = epi.tile([P, S_TOK], F32, name="ut")
-            nc.vector.scalar_tensor_tensor(out=ut[:], in0=accs[h][:], scalar=bias[:, h:h + 1], in1=cos_t[:],
-                                           op0=ALU.add, op1=ALU.mult)
-            uvs[h] = [ut]
-
         def epi_v(h):
-            vt = epi.tile([P, S_TOK], F32, name="vt")
-            nc.vector.scalar_tensor_tensor(out=vt[:], in0=accs[h][:], scalar=bias[:, h:h + 1], in1=sin_t[:],
-                                           op0=ALU.add, op1=ALU.mult)
-            uvs[h].append(vt)
+            uv = epi.tile([P, 2, S_TOK], F32, name="uv")
+            nc.vector.scalar_tensor_tensor(out=uv[:], in0=accs[h][:].unsqueeze(1).to_broadcast([P, 2, S_TOK]),
+                                           scalar=bias[:, h:h + 1], in1=cs_t[:], op0=ALU.add, op1=ALU.mult)
+            uvs[h] = uv
 
         def epi_pe(h):
-            ut, vt = uvs[h]
+            uv = uvs[h]
             o = bank([P, 4, P], "o")
             for a in range(4):
-                nc.tensor.matmul(out=o[:, a, :], lhsT=ut[:, P * a:P * (a + 1)], rhs=ident[:],
+                nc.tensor.matmul(out=o[:, a, :], lhsT=uv[:, 0, P * a:P * (a + 1)], rhs=ident[:],
                                  start=True, stop=False, is_transpose=True)
-                nc.tensor.matmul(out=o[:, a, :], lhsT=vt[:, P * a:P * (a + 1)], rhs=psw[:],
+                nc.tensor.matmul(out=o[:, a, :], lhsT=uv[:, 1, P * a:P * (a + 1)], rhs=psw[:],
                                  start=False, stop=True, is_transpose=True)
             os_[h] = o
 
@@ -199,40 +199,55 @@ def tile_multiheadedattention_pa_kernel(tc, x, w, b, out):
 
         new_block(0, 2)
         new_block(2, 2)
-        for k in range(9):
+
+        def unit(k):
+            return 2 * (k // PASSES), k % PASSES
+
+        def quant_unit(k):
+            first, c = unit(k)
+            quant(first, slice(c, c + 1))
+
+        def mx_unit(k):
+            first, c = unit(k)
+            mx(first, c)
+            mx(first + 1, c)
+
+        for k in range(8):
             if k < PASSES:
                 x_pass(k)
-            if k < 8:
-                interleave(2 * (k // PASSES), slice(k % PASSES, k % PASSES + 1))
-            if k == 6:
-                epi_u(0)
+            first, c = unit(k)
+            interleave(first, slice(c, c + 1))
             if 1 <= k <= PASSES:
                 x_quant(k - 1)
             if k >= 1:
-                first, c = 2 * ((k - 1) // PASSES), (k - 1) % PASSES
-                quant(first, slice(c, c + 1))
-                mx(first, c)
-                mx(first + 1, c)
+                quant_unit(k - 1)
+            if k == PASSES:
+                for kk in range(PASSES):
+                    mx_unit(kk)
+            if k > PASSES:
+                mx_unit(k - 1)
+            if k == 3:
+                nc.scalar.activation(out=cs_t[:, 1, :], in_=fr[:, 0:S_TOK], func=ACT.Sin, scale=fac[:, 0:1])
+                nc.scalar.activation(out=cs_t[:, 0, :], in_=fr[:, S_TOK:], func=ACT.Sin, scale=2.0 * PI)
+            if k >= 6:
+                epi_v(k - 6)
+                epi_pe(k - 6)
             if k == 7:
-                epi_v(0)
-            if k == 2:
-                nc.scalar.activation(out=sin_t[:], in_=fr[:, 0:S_TOK], func=ACT.Sin, scale=fac[:, 0:1])
-                nc.scalar.activation(out=cos_t[:], in_=fr[:, S_TOK:], func=ACT.Sin, scale=2.0 * PI)
+                epi_s(0)
         every = slice(0, PASSES)
-        for t in range(4, H + 6):
+        for t in range(4, H + 4):
+            if t == 4:
+                quant_unit(7)
+                mx_unit(7)
+            elif t - 1 < H:
+                quant(t - 1, every)
+                for c in range(PASSES):
+                    mx(t - 1, c)
             if t < H:
                 new_block(t, 1)
                 interleave(t, every)
+            if t - 2 < H:
+                epi_v(t - 2)
+                epi_pe(t - 2)
             if t - 3 < H:
-                epi_u(t - 3)
-            if 4 <= t - 1 < H:
-                quant(t - 1, every)
-            if t - 3 < H:
-                epi_v(t - 3)
-            if 4 <= t - 2 < H:
-                for c in range(PASSES):
-                    mx(t - 2, c)
-            if t - 4 < H:
-                epi_pe(t - 4)
-            if 0 <= t - 5 < H:
-                epi_s(t - 5)
+                epi_s(t - 3)

@@ -39,9 +39,11 @@ def tile_multiheadedattention_pa_kernel(tc, x, w, b, out):
 
         xv = x.flatten_outer_dims().rearrange("(r a) k -> r a k", a=4)
         xs = []
-        bias = const.tile([P, H], BF16, name="bias")
-        with nc.allow_non_contiguous_dma(reason="bias, one element a partition"):
-            nc.scalar.dma_start(out=bias[:], in_=b.rearrange("(h j) -> j h", j=P))
+        brow = const.tile([P, P], BF16, name="brow")
+        nc.vector.memset(brow[:], 0.0)
+        nc.scalar.dma_start(out=brow[0:H, :], in_=b.rearrange("(h j) -> h j", j=P))
+        brow32 = const.tile([P, P], F32, name="brow32")
+        bias = const.tile([P, H], F32, name="bias")
         wv = w.rearrange("(c p j) d -> c p j d", p=P, j=4)
         wg = []
         place = []
@@ -50,11 +52,11 @@ def tile_multiheadedattention_pa_kernel(tc, x, w, b, out):
             t = wrawp.tile([P, PASSES, 4, GROUP_W[g]], BF16, name="wg%d" % g)
             wg.append(t)
             for c in range(PASSES):
-                nc.sync.dma_start(out=t[:, c, :, :], in_=wv[c, :, :, col0:col0 + GROUP_W[g]])
                 if g == 0:
                     xc = const.tile([P, 4, 512], BF16, name="xs%d" % c)
                     nc.sync.dma_start(out=xc[:], in_=xv[:, :, 512 * c:512 * (c + 1)])
                     xs.append(xc)
+                nc.sync.dma_start(out=t[:, c, :, :], in_=wv[c, :, :, col0:col0 + GROUP_W[g]])
             for o in range(0, GROUP_W[g], P):
                 place.append((g, o))
             col0 += GROUP_W[g]
@@ -182,15 +184,16 @@ def tile_multiheadedattention_pa_kernel(tc, x, w, b, out):
                                            scalar=bias[:, h:h + 1], in1=cs_t[:], op0=ALU.add, op1=ALU.mult)
             uvs[h] = uv
 
-        def epi_pe(h):
+        def epi_pe(h, half):
             uv = uvs[h]
-            o = bank([P, 4, P], "o")
-            for a in range(4):
+            if half == 0:
+                os_[h] = bank([P, 4, P], "o")
+            o = os_[h]
+            for a in range(2 * half, 2 * half + 2):
                 nc.tensor.matmul(out=o[:, a, :], lhsT=uv[:, 0, P * a:P * (a + 1)], rhs=ident[:],
                                  start=True, stop=False, is_transpose=True)
                 nc.tensor.matmul(out=o[:, a, :], lhsT=uv[:, 1, P * a:P * (a + 1)], rhs=psw[:],
                                  start=False, stop=True, is_transpose=True)
-            os_[h] = o
 
         def epi_s(h):
             res = epi.tile([P, S_TOK], F32, name="res")
@@ -221,33 +224,41 @@ def tile_multiheadedattention_pa_kernel(tc, x, w, b, out):
                 x_quant(k - 1)
             if k >= 1:
                 quant_unit(k - 1)
+            if k == 2:
+                nc.vector.tensor_copy(out=brow32[:], in_=brow[:])
+            if k == 3:
+                bt = bank([P, P], "bt")
+                nc.tensor.transpose(bt[:], brow32[:], ident[:])
+                nc.scalar.activation(out=cs_t[:, 1, :], in_=fr[:, 0:S_TOK], func=ACT.Sin, scale=fac[:, 0:1])
+                nc.scalar.activation(out=cs_t[:, 0, :], in_=fr[:, S_TOK:], func=ACT.Sin, scale=2.0 * PI)
             if k == PASSES:
+                nc.vector.tensor_copy(out=bias[:], in_=bt[:, 0:H])
                 for kk in range(PASSES):
                     mx_unit(kk)
             if k > PASSES:
                 mx_unit(k - 1)
-            if k == 3:
-                nc.scalar.activation(out=cs_t[:, 1, :], in_=fr[:, 0:S_TOK], func=ACT.Sin, scale=fac[:, 0:1])
-                nc.scalar.activation(out=cs_t[:, 0, :], in_=fr[:, S_TOK:], func=ACT.Sin, scale=2.0 * PI)
             if k >= 6:
                 epi_v(k - 6)
-                epi_pe(k - 6)
             if k == 7:
-                epi_s(0)
+                epi_pe(0, 0)
+                epi_pe(0, 1)
         every = slice(0, PASSES)
-        for t in range(4, H + 4):
+        for t in range(4, H + 5):
             if t == 4:
                 quant_unit(7)
                 mx_unit(7)
             elif t - 1 < H:
                 quant(t - 1, every)
-                for c in range(PASSES):
-                    mx(t - 1, c)
             if t < H:
                 new_block(t, 1)
                 interleave(t, every)
             if t - 2 < H:
                 epi_v(t - 2)
-                epi_pe(t - 2)
-            if t - 3 < H:
-                epi_s(t - 3)
+            for half in range(2):
+                if t - 3 < H:
+                    epi_pe(t - 3, half)
+                if 4 < t and t - 1 < H:
+                    mx(t - 1, 2 * half)
+                    mx(t - 1, 2 * half + 1)
+            if t - 4 < H:
+                epi_s(t - 4)

@@ -22,7 +22,7 @@ PASSES = 4
 PI = 3.141592653589793
 FLOPS = 2 * S_TOK * K * D
 
-S_W = 90
+S_W = 72
 GROUP_W = (256, 256, 256, 256, 512, 512)
 
 
@@ -43,7 +43,6 @@ def tile_multiheadedattention_pa_kernel(tc, x, w, b, out):
         nc.vector.memset(brow[:], 0.0)
         nc.scalar.dma_start(out=brow[0:H, :], in_=b.rearrange("(h j) -> h j", j=P))
         brow32 = const.tile([P, P], F32, name="brow32")
-        bias = const.tile([P, H], F32, name="bias")
         wv = w.rearrange("(c p j) d -> c p j d", p=P, j=4)
         wg = []
         place = []
@@ -125,8 +124,10 @@ def tile_multiheadedattention_pa_kernel(tc, x, w, b, out):
         uvs = {}
         os_ = {}
 
+        bias = psum.tile([P, P], F32, name="bias", tag="bias", bufs=1)
+
         def bank(shape, name):
-            return psum.tile(shape, F32, name=name, tag="bank", bufs=8)
+            return psum.tile(shape, F32, name=name, tag="bank", bufs=7)
 
         def x_pass(c):
             for ap in range(2):
@@ -156,11 +157,14 @@ def tile_multiheadedattention_pa_kernel(tc, x, w, b, out):
             if cs.stop - cs.start == 1:
                 cut = heads * S_W
                 nc.scalar.copy(out=gw[:, cs, 0:cut, :], in_=src[:, :, :, 0:cut].rearrange("p c j w -> p c w j"))
-                nc.vector.tensor_copy(out=gw[:, cs, cut:, :], in_=src[:, :, :, cut:].rearrange("p c j w -> p c w j"))
+                nc.gpsimd.tensor_scalar(out=gw[:, cs, cut:, :], in0=src[:, :, :, cut:].rearrange("p c j w -> p c w j"),
+                                        scalar1=1.0, scalar2=0.0, op0=ALU.mult, op1=ALU.add)
             else:
-                ns = 2 if h % 4 == 3 else 3
+                ns = 3 if h % 4 == 3 else 2
                 nc.scalar.copy(out=gw[:, 0:ns, :, :], in_=src[:, 0:ns, :, :].rearrange("p c j w -> p c w j"))
-                nc.vector.tensor_copy(out=gw[:, ns:, :, :], in_=src[:, ns:, :, :].rearrange("p c j w -> p c w j"))
+                for c in range(ns, PASSES):
+                    nc.gpsimd.tensor_scalar(out=gw[:, c, :, :], in0=src[:, c, :, :].rearrange("p j w -> p w j"),
+                                            scalar1=1.0, scalar2=0.0, op0=ALU.mult, op1=ALU.add)
 
         def quant(h, cs):
             gw, wq, wsc, first, heads = blocks[h]
@@ -180,8 +184,9 @@ def tile_multiheadedattention_pa_kernel(tc, x, w, b, out):
 
         def epi_v(h):
             uv = epi.tile([P, 2, S_TOK], F32, name="uv")
-            nc.vector.scalar_tensor_tensor(out=uv[:], in0=accs[h][:].unsqueeze(1).to_broadcast([P, 2, S_TOK]),
-                                           scalar=bias[:, h:h + 1], in1=cs_t[:], op0=ALU.add, op1=ALU.mult)
+            for e in range(2):
+                nc.vector.scalar_tensor_tensor(out=uv[:, e, :], in0=accs[h][:], scalar=bias[:, h:h + 1],
+                                               in1=cs_t[:, e, :], op0=ALU.add, op1=ALU.mult)
             uvs[h] = uv
 
         def epi_pe(h, half):
@@ -196,7 +201,7 @@ def tile_multiheadedattention_pa_kernel(tc, x, w, b, out):
                                  start=False, stop=True, is_transpose=True)
 
         def epi_s(h):
-            res = epi.tile([P, S_TOK], F32, name="res")
+            res = epi.tile([P, S_TOK], F32, name="res", bufs=6)
             nc.scalar.copy(out=res[:], in_=os_[h][:].rearrange("p a j -> p (a j)"))
             nc.sync.dma_start(out=outv[h], in_=res[:])
 
@@ -227,12 +232,10 @@ def tile_multiheadedattention_pa_kernel(tc, x, w, b, out):
             if k == 2:
                 nc.vector.tensor_copy(out=brow32[:], in_=brow[:])
             if k == 3:
-                bt = bank([P, P], "bt")
-                nc.tensor.transpose(bt[:], brow32[:], ident[:])
+                nc.tensor.transpose(bias[:], brow32[:], ident[:])
                 nc.scalar.activation(out=cs_t[:, 1, :], in_=fr[:, 0:S_TOK], func=ACT.Sin, scale=fac[:, 0:1])
                 nc.scalar.activation(out=cs_t[:, 0, :], in_=fr[:, S_TOK:], func=ACT.Sin, scale=2.0 * PI)
             if k == PASSES:
-                nc.vector.tensor_copy(out=bias[:], in_=bt[:, 0:H])
                 for kk in range(PASSES):
                     mx_unit(kk)
             if k > PASSES:
@@ -254,11 +257,11 @@ def tile_multiheadedattention_pa_kernel(tc, x, w, b, out):
                 interleave(t, every)
             if t - 2 < H:
                 epi_v(t - 2)
-            for half in range(2):
-                if t - 3 < H:
-                    epi_pe(t - 3, half)
-                if 4 < t and t - 1 < H:
-                    mx(t - 1, 2 * half)
-                    mx(t - 1, 2 * half + 1)
+            if t - 3 < H:
+                epi_pe(t - 3, 0)
+                epi_pe(t - 3, 1)
+            if 4 < t and t - 1 < H:
+                for c in range(PASSES):
+                    mx(t - 1, c)
             if t - 4 < H:
                 epi_s(t - 4)

@@ -144,9 +144,10 @@ def tile_multiheadedattention_pa_kernel(tc, x, w, b, out):
             nc.vector.quantize_mx(out=xq[:, c, :].bitcast(E5X4), scales=xsc[:, c, :], in_=gx[c][:])
 
         def new_block(first, heads):
-            gw = gwp.tile([P, PASSES, heads * P, 4], BF16, name="gw%d" % heads, align_bytes=64)
-            wq = wqp.tile([P, PASSES, heads * P], U32, name="wq%d" % heads, align_bytes=64)
-            wsc = wqp.tile([P, PASSES, heads * P], U8, name="wsc%d" % heads, align_bytes=64)
+            nb = 2 if heads == 2 else 4
+            gw = gwp.tile([P, PASSES, heads * P, 4], BF16, name="gw%d" % heads, align_bytes=64, bufs=nb)
+            wq = wqp.tile([P, PASSES, heads * P], U32, name="wq%d" % heads, align_bytes=64, bufs=nb)
+            wsc = wqp.tile([P, PASSES, heads * P], U8, name="wsc%d" % heads, align_bytes=64, bufs=nb)
             for i in range(heads):
                 blocks[first + i] = (gw, wq, wsc, first, heads)
 
@@ -183,7 +184,7 @@ def tile_multiheadedattention_pa_kernel(tc, x, w, b, out):
                                 start=(c == 0), stop=(c == PASSES - 1))
 
         def epi_v(h):
-            uv = epi.tile([P, 2, S_TOK], F32, name="uv")
+            uv = epi.tile([P, 2, S_TOK], F32, name="uv", bufs=5)
             for e in range(2):
                 nc.vector.scalar_tensor_tensor(out=uv[:, e, :], in0=accs[h][:], scalar=bias[:, h:h + 1],
                                                in1=cs_t[:, e, :], op0=ALU.add, op1=ALU.mult)
@@ -246,22 +247,30 @@ def tile_multiheadedattention_pa_kernel(tc, x, w, b, out):
                 epi_pe(0, 0)
                 epi_pe(0, 1)
         every = slice(0, PASSES)
-        for t in range(4, H + 5):
-            if t == 4:
+        for a in range(4, H + 6, 2):
+            pair = (a, a + 1)
+            for h in pair:
+                if h < H:
+                    new_block(h, 1)
+                    interleave(h, every)
+            if a == 4:
                 quant_unit(7)
+            for h in pair:
+                if 4 <= h - 2 < H:
+                    quant(h - 2, every)
+            for h in pair:
+                if 2 <= h - 4 < H:
+                    epi_v(h - 4)
+            for h in pair:
+                if 1 <= h - 6 < H:
+                    epi_pe(h - 6, 0)
+                    epi_pe(h - 6, 1)
+            if a == 4:
                 mx_unit(7)
-            elif t - 1 < H:
-                quant(t - 1, every)
-            if t < H:
-                new_block(t, 1)
-                interleave(t, every)
-            if t - 2 < H:
-                epi_v(t - 2)
-            if t - 3 < H:
-                epi_pe(t - 3, 0)
-                epi_pe(t - 3, 1)
-            if 4 < t and t - 1 < H:
-                for c in range(PASSES):
-                    mx(t - 1, c)
-            if t - 4 < H:
-                epi_s(t - 4)
+            for h in pair:
+                if 4 <= h - 2 < H:
+                    for c in range(PASSES):
+                        mx(h - 2, c)
+            for h in pair:
+                if 0 <= h - 6 < H:
+                    epi_s(h - 6)

@@ -161,7 +161,7 @@ def tile_multiheadedattention_pa_kernel(tc, x, w, b, out):
                 nc.gpsimd.tensor_scalar(out=gw[:, cs, cut:, :], in0=src[:, :, :, cut:].rearrange("p c j w -> p c w j"),
                                         scalar1=1.0, scalar2=0.0, op0=ALU.mult, op1=ALU.add)
             else:
-                ns = 3 if h % 4 == 3 else 2
+                ns = 3 if h % 2 == 1 else 2
                 nc.scalar.copy(out=gw[:, 0:ns, :, :], in_=src[:, 0:ns, :, :].rearrange("p c j w -> p c w j"))
                 for c in range(ns, PASSES):
                     nc.gpsimd.tensor_scalar(out=gw[:, c, :, :], in0=src[:, c, :, :].rearrange("p j w -> p w j"),

@@ -22,8 +22,8 @@ PASSES = 4
 PI = 3.141592653589793
 FLOPS = 2 * S_TOK * K * D
 
-S_W = 72
-GROUP_W = (256, 256, 256, 256, 512, 512)
+CFG = dict(unit=(("S", 256), ("G", 128), ("V", 128)), even="SSGG", odd="SSSG", mxlag=2, xv=0, sin_at=3)
+GROUP_W = (512, 512, 512, 512)
 
 
 def tile_multiheadedattention_pa_kernel(tc, x, w, b, out):
@@ -138,34 +138,52 @@ def tile_multiheadedattention_pa_kernel(tc, x, w, b, out):
                         nc.tensor.transpose(xt[:, a2, uu, :], words[:, uu:256:2], ident[:])
                 dst = gx[c][:].bitcast(F32)[:, 512 * ap:512 * (ap + 1)].rearrange("p (a r u) -> p a r u", a=2, u=2)
                 src = xt[:].rearrange("p a u r -> p a r u")
-                nc.scalar.copy(out=dst, in_=src)
+                if ap < CFG["xv"]:
+                    nc.vector.tensor_copy(out=dst, in_=src)
+                else:
+                    nc.scalar.copy(out=dst, in_=src)
 
         def x_quant(c):
             nc.vector.quantize_mx(out=xq[:, c, :].bitcast(E5X4), scales=xsc[:, c, :], in_=gx[c][:])
 
         def new_block(first, heads):
-            nb = 2 if heads == 2 else 4
+            nb = 1 if heads == 4 else 4
             gw = gwp.tile([P, PASSES, heads * P, 4], BF16, name="gw%d" % heads, align_bytes=64, bufs=nb)
             wq = wqp.tile([P, PASSES, heads * P], U32, name="wq%d" % heads, align_bytes=64, bufs=nb)
             wsc = wqp.tile([P, PASSES, heads * P], U8, name="wsc%d" % heads, align_bytes=64, bufs=nb)
             for i in range(heads):
                 blocks[first + i] = (gw, wq, wsc, first, heads)
 
-        def interleave(h, cs):
+        def il_copy(eng, dst, src_, pat):
+            view = src_.rearrange(pat)
+            if eng == "S":
+                nc.scalar.copy(out=dst, in_=view)
+            elif eng == "V":
+                nc.vector.tensor_copy(out=dst, in_=view)
+            else:
+                nc.gpsimd.tensor_scalar(out=dst, in0=view, scalar1=1.0, scalar2=0.0, op0=ALU.mult, op1=ALU.add)
+
+        def interleave(h, cs, only=None):
             gw, wq, wsc, first, heads = blocks[h]
             g, o = place[first]
             src = wg[g][:, cs, :, o:o + heads * P]
             if cs.stop - cs.start == 1:
-                cut = heads * S_W
-                nc.scalar.copy(out=gw[:, cs, 0:cut, :], in_=src[:, :, :, 0:cut].rearrange("p c j w -> p c w j"))
-                nc.gpsimd.tensor_scalar(out=gw[:, cs, cut:, :], in0=src[:, :, :, cut:].rearrange("p c j w -> p c w j"),
-                                        scalar1=1.0, scalar2=0.0, op0=ALU.mult, op1=ALU.add)
+                lo = 0
+                for eng, wd in CFG["unit"]:
+                    if only is None or eng in only:
+                        il_copy(eng, gw[:, cs, lo:lo + wd, :], src[:, :, :, lo:lo + wd], "p c j w -> p c w j")
+                    lo += wd
             else:
-                ns = 3 if h % 2 == 1 else 2
-                nc.scalar.copy(out=gw[:, 0:ns, :, :], in_=src[:, 0:ns, :, :].rearrange("p c j w -> p c w j"))
-                for c in range(ns, PASSES):
-                    nc.gpsimd.tensor_scalar(out=gw[:, c, :, :], in0=src[:, c, :, :].rearrange("p j w -> p w j"),
-                                            scalar1=1.0, scalar2=0.0, op0=ALU.mult, op1=ALU.add)
+                plan = CFG["odd"] if h % 2 == 1 else CFG["even"]
+                c = 0
+                while c < PASSES:
+                    e = c + 1
+                    if plan[c] == "S":
+                        while e < PASSES and plan[e] == "S":
+                            e += 1
+                    if only is None or plan[c] in only:
+                        il_copy(plan[c], gw[:, c:e, :, :], src[:, c:e, :, :], "p c j w -> p c w j")
+                    c = e
 
         def quant(h, cs):
             gw, wq, wsc, first, heads = blocks[h]
@@ -206,46 +224,46 @@ def tile_multiheadedattention_pa_kernel(tc, x, w, b, out):
             nc.scalar.copy(out=res[:], in_=os_[h][:].rearrange("p a j -> p (a j)"))
             nc.sync.dma_start(out=outv[h], in_=res[:])
 
-        new_block(0, 2)
-        new_block(2, 2)
+        new_block(0, 4)
 
-        def unit(k):
-            return 2 * (k // PASSES), k % PASSES
+        def quant_unit(c):
+            quant(0, slice(c, c + 1))
 
-        def quant_unit(k):
-            first, c = unit(k)
-            quant(first, slice(c, c + 1))
+        def mx_unit(c):
+            for h in range(4):
+                mx(h, c)
 
-        def mx_unit(k):
-            first, c = unit(k)
-            mx(first, c)
-            mx(first + 1, c)
+        def sin_tables():
+            nc.scalar.activation(out=cs_t[:, 1, :], in_=fr[:, 0:S_TOK], func=ACT.Sin, scale=fac[:, 0:1])
+            nc.scalar.activation(out=cs_t[:, 0, :], in_=fr[:, S_TOK:], func=ACT.Sin, scale=2.0 * PI)
 
-        for k in range(8):
+        done_units = []
+        lag = CFG["mxlag"]
+        if CFG["sin_at"] < 0:
+            sin_tables()
+        for k in range(PASSES + 1 + lag):
             if k < PASSES:
                 x_pass(k)
-            first, c = unit(k)
-            interleave(first, slice(c, c + 1))
+                interleave(0, slice(k, k + 1), "SG")
             if 1 <= k <= PASSES:
                 x_quant(k - 1)
-            if k >= 1:
                 quant_unit(k - 1)
+            if k < PASSES:
+                interleave(0, slice(k, k + 1), "V")
             if k == 2:
                 nc.vector.tensor_copy(out=brow32[:], in_=brow[:])
             if k == 3:
                 nc.tensor.transpose(bias[:], brow32[:], ident[:])
-                nc.scalar.activation(out=cs_t[:, 1, :], in_=fr[:, 0:S_TOK], func=ACT.Sin, scale=fac[:, 0:1])
-                nc.scalar.activation(out=cs_t[:, 0, :], in_=fr[:, S_TOK:], func=ACT.Sin, scale=2.0 * PI)
-            if k == PASSES:
-                for kk in range(PASSES):
-                    mx_unit(kk)
-            if k > PASSES:
-                mx_unit(k - 1)
-            if k >= 6:
-                epi_v(k - 6)
-            if k == 7:
-                epi_pe(0, 0)
-                epi_pe(0, 1)
+            if k == CFG["sin_at"]:
+                sin_tables()
+            if k >= PASSES:
+                for kk in range(max(0, PASSES - lag), PASSES):
+                    if kk not in done_units and kk + 1 <= k:
+                        done_units.append(kk)
+                        mx_unit(kk)
+            elif 0 <= k - lag:
+                done_units.append(k - lag)
+                mx_unit(k - lag)
         every = slice(0, PASSES)
         for a in range(4, H + 6, 2):
             pair = (a, a + 1)
@@ -253,20 +271,16 @@ def tile_multiheadedattention_pa_kernel(tc, x, w, b, out):
                 if h < H:
                     new_block(h, 1)
                     interleave(h, every)
-            if a == 4:
-                quant_unit(7)
             for h in pair:
                 if 4 <= h - 2 < H:
                     quant(h - 2, every)
             for h in pair:
-                if 2 <= h - 4 < H:
+                if 0 <= h - 4 < H:
                     epi_v(h - 4)
             for h in pair:
-                if 1 <= h - 6 < H:
+                if 0 <= h - 6 < H:
                     epi_pe(h - 6, 0)
                     epi_pe(h - 6, 1)
-            if a == 4:
-                mx_unit(7)
             for h in pair:
                 if 4 <= h - 2 < H:
                     for c in range(PASSES):

@@ -155,13 +155,16 @@ def tile_multiheadedattention_pa_kernel(tc, x, w, b, out):
                 blocks[first + i] = (gw, wq, wsc, first, heads)
 
         def il_copy(eng, dst, src_, pat):
-            view = src_.rearrange(pat)
-            if eng == "S":
-                nc.scalar.copy(out=dst, in_=view)
-            elif eng == "V":
-                nc.vector.tensor_copy(out=dst, in_=view)
-            else:
-                nc.gpsimd.tensor_scalar(out=dst, in0=view, scalar1=1.0, scalar2=0.0, op0=ALU.mult, op1=ALU.add)
+            if eng == "V":
+                nc.vector.tensor_copy(out=dst, in_=src_.rearrange(pat))
+                return
+            for c in range(dst.shape[1]):
+                d4 = dst[:, c, :, :].rearrange("p (q i) t -> p q t i", i=4)
+                s4 = src_[:, c, :, :].rearrange("p t (q i) -> p q t i", i=4)
+                if eng == "S":
+                    nc.scalar.copy(out=d4, in_=s4)
+                else:
+                    nc.gpsimd.tensor_scalar(out=d4, in0=s4, scalar1=1.0, scalar2=0.0, op0=ALU.mult, op1=ALU.add)
 
         def interleave(h, cs, only=None):
             gw, wq, wsc, first, heads = blocks[h]

@@ -22,7 +22,7 @@ PASSES = 4
 PI = 3.141592653589793
 FLOPS = 2 * S_TOK * K * D
 
-CFG = dict(unit=(("S", 256), ("G", 128), ("V", 128)), even="SSGG", odd="SSSG", mxlag=2, xv=0, sin_at=3)
+CFG = dict(unit=(("S", 224), ("V", 288)), even="SSGG", odd="SSSG", mxlag=2, xv=0, sin_at=3)
 GROUP_W = (512, 512, 512, 512)
 
 

from contextlib import ExitStack

import concourse.mybir as mybir
from concourse.masks import make_identity

F32 = mybir.dt.float32
BF16 = mybir.dt.bfloat16
I32 = mybir.dt.int32
U32 = mybir.dt.uint32
U8 = mybir.dt.uint8
E4X4 = mybir.dt.float8_e4m3fn_x4
E5X4 = mybir.dt.float8_e5m2_x4
ALU = mybir.AluOpType
ACT = mybir.ActivationFunctionType

P = 128
S_TOK = 512
K = 2048
D = 2048
H = 16
PASSES = 4
PI = 3.141592653589793
FLOPS = 2 * S_TOK * K * D

CFG = dict(unit=(("S", 224), ("V", 288)), even="SSGG", odd="SSSG", mxlag=2, xv=0, sin_at=3)
GROUP_W = (512, 512, 512, 512)


def tile_multiheadedattention_pa_kernel(tc, x, w, b, out):
    nc = tc.nc
    with ExitStack() as ctx:
        const = ctx.enter_context(tc.tile_pool(name="const", bufs=1))
        wrawp = ctx.enter_context(tc.tile_pool(name="wrawp", bufs=1))
        gwp = ctx.enter_context(tc.tile_pool(name="gwp", bufs=3))
        wqp = ctx.enter_context(tc.tile_pool(name="wqp", bufs=3))
        epi = ctx.enter_context(tc.tile_pool(name="epi", bufs=3))
        psum = ctx.enter_context(tc.psum_pool(name="psum", bufs=1))
        ctx.enter_context(tc.manual_schedule())

        xv = x.flatten_outer_dims().rearrange("(r a) k -> r a k", a=4)
        xs = []
        brow = const.tile([P, P], BF16, name="brow")
        nc.vector.memset(brow[:], 0.0)
        nc.scalar.dma_start(out=brow[0:H, :], in_=b.rearrange("(h j) -> h j", j=P))
        brow32 = const.tile([P, P], F32, name="brow32")
        wv = w.rearrange("(c p j) d -> c p j d", p=P, j=4)
        wg = []
        place = []
        col0 = 0
        for g in range(len(GROUP_W)):
            t = wrawp.tile([P, PASSES, 4, GROUP_W[g]], BF16, name="wg%d" % g)
            wg.append(t)
            for c in range(PASSES):
                if g == 0:
                    xc = const.tile([P, 4, 512], BF16, name="xs%d" % c)
                    nc.sync.dma_start(out=xc[:], in_=xv[:, :, 512 * c:512 * (c + 1)])
                    xs.append(xc)
                nc.sync.dma_start(out=t[:, c, :, :], in_=wv[c, :, :, col0:col0 + GROUP_W[g]])
            for o in range(0, GROUP_W[g], P):
                place.append((g, o))
            col0 += GROUP_W[g]

        zero1 = const.tile([P, 1], F32, name="zero1")
        nc.vector.memset(zero1[:], 0.0)
        warm = const.tile([P, 1], F32, name="warm")
        nc.scalar.activation(out=warm[:], in_=zero1[:], func=ACT.Sin)

        jcol = const.tile([P, 1], I32, name="jcol")
        nc.gpsimd.iota(jcol[:], pattern=[[0, 1]], base=0, channel_multiplier=1)
        mi = const.tile([P, S_TOK], F32, name="mi")
        nc.gpsimd.iota(mi[:], pattern=[[1, 4], [4, P]], base=0, channel_multiplier=0,
                       allow_small_or_imprecise_dtypes=True)
        ident = const.tile([P, P], F32, name="ident")
        make_identity(nc, ident[:])
        psw = const.tile([P, P], F32, name="psw")
        iv = ident[:].rearrange("p (i e) -> p i e", e=2)
        pv = psw[:].rearrange("p (i e) -> p i e", e=2)
        nc.gpsimd.tensor_copy(out=pv[:, :, 0:1], in_=iv[:, :, 1:2])
        nc.gpsimd.tensor_copy(out=pv[:, :, 1:2], in_=iv[:, :, 0:1])

        bits = const.tile([P, 8], I32, name="bits")
        for k in range(7):
            nc.vector.tensor_scalar(out=bits[:, k:k + 1], in0=jcol[:], scalar1=k, scalar2=1,
                                    op0=ALU.logical_shift_right, op1=ALU.bitwise_and)
        bitsf = const.tile([P, 8], F32, name="bitsf")
        nc.vector.tensor_copy(out=bitsf[:, 0:7], in_=bits[:, 0:7])
        fac = const.tile([P, 8], F32, name="fac")
        for k in range(1, 7):
            ck = 10.0 ** (-(2.0 ** (k - 1)) / 16.0)
            s0 = 1.0 / (2.0 * PI) if k == 1 else 1.0
            nc.vector.tensor_scalar(out=fac[:, k:k + 1], in0=bitsf[:, k:k + 1], scalar1=(ck - 1.0) * s0,
                                    scalar2=s0, op0=ALU.mult, op1=ALU.add)
        nc.vector.tensor_scalar(out=fac[:, 0:1], in0=bitsf[:, 0:1], scalar1=-4.0 * PI, scalar2=2.0 * PI,
                                op0=ALU.mult, op1=ALU.add)
        turns = const.tile([P, 4], F32, name="turns")
        nc.vector.tensor_scalar(out=turns[:, 0:1], in0=fac[:, 1:2], scalar1=fac[:, 2:3], scalar2=fac[:, 3:4],
                                op0=ALU.mult, op1=ALU.mult)
        nc.vector.tensor_scalar(out=turns[:, 1:2], in0=turns[:, 0:1], scalar1=fac[:, 4:5], scalar2=fac[:, 5:6],
                                op0=ALU.mult, op1=ALU.mult)
        nc.vector.tensor_scalar(out=turns[:, 2:3], in0=turns[:, 1:2], scalar1=fac[:, 6:7], scalar2=None,
                                op0=ALU.mult)
        u = turns[:, 2:3]

        fr = const.tile([P, 2 * S_TOK], F32, name="fr")
        ni = const.tile([P, 2 * S_TOK], I32, name="ni")
        nf = const.tile([P, 2 * S_TOK], F32, name="nf")
        for e in range(2):
            half = slice(S_TOK * e, S_TOK * (e + 1))
            nc.vector.tensor_scalar(out=ni[:, half], in0=mi[:], scalar1=u, scalar2=0.25 * e, op0=ALU.mult, op1=ALU.add)
            nc.vector.tensor_scalar(out=nf[:, half], in0=ni[:, half], scalar1=-0.25 * e, scalar2=None, op0=ALU.add)
            nc.vector.scalar_tensor_tensor(out=fr[:, half], in0=mi[:], scalar=u, in1=nf[:, half],
                                           op0=ALU.mult, op1=ALU.subtract)
        cs_t = const.tile([P, 2, S_TOK], F32, name="cs_t")

        gx = []
        for c in range(PASSES):
            g = const.tile([P, 4 * S_TOK], BF16, name="gx%d" % c, align_bytes=64)
            gx.append(g)
        xq = const.tile([P, PASSES, S_TOK], U32, name="xq", align_bytes=64)
        xsc = const.tile([P, PASSES, S_TOK], U8, name="xsc", align_bytes=64)
        outv = out.rearrange("o h (r a) j -> (o h) r (a j)", a=4)
        blocks = {}
        accs = {}
        uvs = {}
        os_ = {}

        bias = psum.tile([P, P], F32, name="bias", tag="bias", bufs=1)

        def bank(shape, name):
            return psum.tile(shape, F32, name=name, tag="bank", bufs=7)

        def x_pass(c):
            for ap in range(2):
                xt = bank([P, 2, 2, P], "xt")
                for a2 in range(2):
                    words = xs[c][:, 2 * ap + a2, :].bitcast(F32)
                    for uu in range(2):
                        nc.tensor.transpose(xt[:, a2, uu, :], words[:, uu:256:2], ident[:])
                dst = gx[c][:].bitcast(F32)[:, 512 * ap:512 * (ap + 1)].rearrange("p (a r u) -> p a r u", a=2, u=2)
                src = xt[:].rearrange("p a u r -> p a r u")
                if ap < CFG["xv"]:
                    nc.vector.tensor_copy(out=dst, in_=src)
                else:
                    nc.scalar.copy(out=dst, in_=src)

        def x_quant(c):
            nc.vector.quantize_mx(out=xq[:, c, :].bitcast(E5X4), scales=xsc[:, c, :], in_=gx[c][:])

        def new_block(first, heads):
            nb = 1 if heads == 4 else 4
            gw = gwp.tile([P, PASSES, heads * P, 4], BF16, name="gw%d" % heads, align_bytes=64, bufs=nb)
            wq = wqp.tile([P, PASSES, heads * P], U32, name="wq%d" % heads, align_bytes=64, bufs=nb)
            wsc = wqp.tile([P, PASSES, heads * P], U8, name="wsc%d" % heads, align_bytes=64, bufs=nb)
            for i in range(heads):
                blocks[first + i] = (gw, wq, wsc, first, heads)

        def il_copy(eng, dst, src_, pat):
            if eng == "V":
                nc.vector.tensor_copy(out=dst, in_=src_.rearrange(pat))
                return
            for c in range(dst.shape[1]):
                d4 = dst[:, c, :, :].rearrange("p (q i) t -> p q t i", i=4)
                s4 = src_[:, c, :, :].rearrange("p t (q i) -> p q t i", i=4)
                if eng == "S":
                    nc.scalar.copy(out=d4, in_=s4)
                else:
                    nc.gpsimd.tensor_scalar(out=d4, in0=s4, scalar1=1.0, scalar2=0.0, op0=ALU.mult, op1=ALU.add)

        def interleave(h, cs, only=None):
            gw, wq, wsc, first, heads = blocks[h]
            g, o = place[first]
            src = wg[g][:, cs, :, o:o + heads * P]
            if cs.stop - cs.start == 1:
                lo = 0
                for eng, wd in CFG["unit"]:
                    if only is None or eng in only:
                        il_copy(eng, gw[:, cs, lo:lo + wd, :], src[:, :, :, lo:lo + wd], "p c j w -> p c w j")
                    lo += wd
            else:
                plan = CFG["odd"] if h % 2 == 1 else CFG["even"]
                c = 0
                while c < PASSES:
                    e = c + 1
                    if plan[c] == "S":
                        while e < PASSES and plan[e] == "S":
                            e += 1
                    if only is None or plan[c] in only:
                        il_copy(plan[c], gw[:, c:e, :, :], src[:, c:e, :, :], "p c j w -> p c w j")
                    c = e

        def quant(h, cs):
            gw, wq, wsc, first, heads = blocks[h]
            nc.vector.quantize_mx(out=wq[:, cs, :].rearrange("p c w -> p (c w)").bitcast(E4X4),
                                  scales=wsc[:, cs, :].rearrange("p c w -> p (c w)"),
                                  in_=gw[:, cs, :, :].rearrange("p c w j -> p (c w j)"))

        def mx(h, c):
            gw, wq, wsc, first, heads = blocks[h]
            cols = slice(P * (h - first), P * (h - first + 1))
            if c == 0:
                accs[h] = bank([P, S_TOK], "acc")
            nc.tensor.matmul_mx(out=accs[h][:],
                                lhsT=wq[:, c, cols].bitcast(E4X4), lhsT_scale=wsc[:, c, cols],
                                rhs=xq[:, c, :].bitcast(E5X4), rhs_scale=xsc[:, c, :],
                                start=(c == 0), stop=(c == PASSES - 1))

        def epi_v(h):
            uv = epi.tile([P, 2, S_TOK], F32, name="uv", bufs=5)
            for e in range(2):
                nc.vector.scalar_tensor_tensor(out=uv[:, e, :], in0=accs[h][:], scalar=bias[:, h:h + 1],
                                               in1=cs_t[:, e, :], op0=ALU.add, op1=ALU.mult)
            uvs[h] = uv

        def epi_pe(h, half):
            uv = uvs[h]
            if half == 0:
                os_[h] = bank([P, 4, P], "o")
            o = os_[h]
            for a in range(2 * half, 2 * half + 2):
                nc.tensor.matmul(out=o[:, a, :], lhsT=uv[:, 0, P * a:P * (a + 1)], rhs=ident[:],
                                 start=True, stop=False, is_transpose=True)
                nc.tensor.matmul(out=o[:, a, :], lhsT=uv[:, 1, P * a:P * (a + 1)], rhs=psw[:],
                                 start=False, stop=True, is_transpose=True)

        def epi_s(h):
            res = epi.tile([P, S_TOK], F32, name="res", bufs=6)
            nc.scalar.copy(out=res[:], in_=os_[h][:].rearrange("p a j -> p (a j)"))
            nc.sync.dma_start(out=outv[h], in_=res[:])

        new_block(0, 4)

        def quant_unit(c):
            quant(0, slice(c, c + 1))

        def mx_unit(c):
            for h in range(4):
                mx(h, c)

        def sin_tables():
            nc.scalar.activation(out=cs_t[:, 1, :], in_=fr[:, 0:S_TOK], func=ACT.Sin, scale=fac[:, 0:1])
            nc.scalar.activation(out=cs_t[:, 0, :], in_=fr[:, S_TOK:], func=ACT.Sin, scale=2.0 * PI)

        done_units = []
        lag = CFG["mxlag"]
        if CFG["sin_at"] < 0:
            sin_tables()
        for k in range(PASSES + 1 + lag):
            if k < PASSES:
                x_pass(k)
                interleave(0, slice(k, k + 1), "SG")
            if 1 <= k <= PASSES:
                x_quant(k - 1)
                quant_unit(k - 1)
            if k < PASSES:
                interleave(0, slice(k, k + 1), "V")
            if k == 2:
                nc.vector.tensor_copy(out=brow32[:], in_=brow[:])
            if k == 3:
                nc.tensor.transpose(bias[:], brow32[:], ident[:])
            if k == CFG["sin_at"]:
                sin_tables()
            if k >= PASSES:
                for kk in range(max(0, PASSES - lag), PASSES):
                    if kk not in done_units and kk + 1 <= k:
                        done_units.append(kk)
                        mx_unit(kk)
            elif 0 <= k - lag:
                done_units.append(k - lag)
                mx_unit(k - lag)
        every = slice(0, PASSES)
        for a in range(4, H + 6, 2):
            pair = (a, a + 1)
            for h in pair:
                if h < H:
                    new_block(h, 1)
                    interleave(h, every)
            for h in pair:
                if 4 <= h - 2 < H:
                    quant(h - 2, every)
            for h in pair:
                if 0 <= h - 4 < H:
                    epi_v(h - 4)
            for h in pair:
                if 0 <= h - 6 < H:
                    epi_pe(h - 6, 0)
                    epi_pe(h - 6, 1)
            for h in pair:
                if 4 <= h - 2 < H:
                    for c in range(PASSES):
                        mx(h - 2, c)
            for h in pair:
                if 0 <= h - 6 < H:
                    epi_s(h - 6)
